import numpy as np
import ml_dtypes


def mxq(x, axis, fmt="e4m3"):
    dtype, down = {"e4m3": (ml_dtypes.float8_e4m3fn, 7), "e5m2": (ml_dtypes.float8_e5m2, 14)}[fmt]
    v = np.moveaxis(np.asarray(x, np.float32).astype(ml_dtypes.bfloat16).astype(np.float64), axis, -1)
    blocks = v.reshape(v.shape[:-1] + (-1, 32))
    amax = np.abs(blocks).max(-1, keepdims=True)
    byte = np.maximum(np.where(amax > 0, np.frexp(amax)[1] - 1 + 127, 0) - down, 1)
    scale = np.exp2(byte - 127.0)
    codes = (blocks / scale).astype(np.float32).astype(dtype).astype(np.float64)
    return np.moveaxis((codes * scale).reshape(v.shape), -1, axis)


WIDE = False


def mx_kscale(k):
    if not WIDE:
        return np.ones(k)
    levels = np.array([30, -30])
    if k % 512:
        return np.exp2(np.random.permutation(np.resize(levels, k // 32))).repeat(32)
    a = np.empty((k // 512, 16))
    for p in range(k // 512):
        a[p, :8] = np.random.permutation(np.resize(levels, 8))
        for g in range(8):
            far = levels[np.abs(levels - a[p, g]) >= 10]
            a[p, g + 8] = far[np.random.randint(len(far))]
    return np.exp2(a.ravel()).repeat(32)


BF16 = ml_dtypes.bfloat16


def bf(x):
    return np.asarray(x, np.float32).astype(BF16)


def f64(x):
    return np.asarray(x).astype(np.float64)


B, S, IN, OUT, A, R = 8, 128, 2048, 2048, 8, 128
G = B // A
SCALING = 2.0


def setup_inputs():
    s = mx_kscale(IN)
    return {"data": bf(np.random.standard_normal((B, S, IN)) * s),
            "W": bf(np.random.standard_normal((OUT, IN)) / np.sqrt(IN) / s),
            "t_lora": bf(np.random.standard_normal((A, G, S, R))),
            "lora_b": bf(np.random.standard_normal((A, OUT, R)) * 0.5 / np.sqrt(R))}


def reference(data, W, t_lora, lora_b):
    base = mxq(f64(data), 2, "e5m2") @ mxq(f64(W), 1, "e5m2").T
    delta = (f64(t_lora).reshape(A, G * S, R) @ f64(lora_b).transpose(0, 2, 1)) * SCALING
    return base + delta.reshape(B, S, OUT)

@@ -1,0 +1,245 @@
+from contextlib import ExitStack
+
+import concourse.mybir as mybir
+from concourse.masks import make_identity
+
+F32 = mybir.dt.float32
+BF16 = mybir.dt.bfloat16
+U32 = mybir.dt.uint32
+U8 = mybir.dt.uint8
+E5X4 = mybir.dt.float8_e5m2_x4
+COPY = mybir.ActivationFunctionType.Copy
+ADD = mybir.AluOpType.add
+
+P = 128
+NT = 8
+NC = 4
+NG = 4
+IN = 2048
+OUT = 2048
+FLOPS = 2 * 1024 * 2048 * 2048 + 2 * 1024 * 2048 * 128
+
+BUFS = {"w": 10, "x": 4, "l": 6, "t": 1}
+
+
+def build_rounds():
+    rounds = []
+    rounds.append(([("W", 0, g, 0) for g in range(NG)], []))
+    rounds.append(([("W", 0, g, 1) for g in range(NG)], []))
+    rounds.append(([("D", 0, 0), ("D", 0, 1), ("T",), ("L", 0, 0)], []))
+    for m in range(NT):
+        bus = []
+        if m + 1 < NT:
+            bus += [("D", m + 1, 0), ("D", m + 1, 1), ("L", m + 1, 0)]
+        bus.append(("W", 1, m % NG, m // NG))
+        rounds.append((bus, [(0, m)]))
+    for q in range(4):
+        bus = [("W", 2, (2 * q) % NG, (2 * q) // NG), ("W", 2, (2 * q + 1) % NG, (2 * q + 1) // NG)]
+        bus += [("L", 2 * q, 1), ("L", 2 * q + 1, 1)]
+        rounds.append((bus, [(1, 2 * q), (1, 2 * q + 1)]))
+    for q in range(4):
+        bus = [("W", 3, (2 * q) % NG, (2 * q) // NG), ("W", 3, (2 * q + 1) % NG, (2 * q + 1) // NG)]
+        rounds.append((bus, [(2, 2 * q), (2, 2 * q + 1)]))
+    rounds.append(([], [(3, m) for m in range(NT)]))
+    return rounds
+
+
+def loads_of(bu):
+    if bu[0] == "W":
+        return [("w", bu[1], 2 * bu[3]), ("w", bu[1], 2 * bu[3] + 1)]
+    if bu[0] == "D":
+        return [("x", bu[1])]
+    if bu[0] == "L":
+        return [("l", bu[1], bu[2])]
+    return [("t",)]
+
+
+def tile_linear_pa_kernel(tc, data, W, t_lora, lora_b, out):
+    nc = tc.nc
+    rounds = build_rounds()
+
+    order = []
+    last_use = {}
+    for r, (bus, units) in enumerate(rounds):
+        for bu in bus:
+            for ld in loads_of(bu):
+                if ld not in last_use:
+                    order.append(ld)
+                last_use[ld] = r
+    by_kind = {"w": [], "x": [], "l": [], "t": []}
+    for ld in order:
+        by_kind[ld[0]].append(ld)
+
+    with ExitStack() as ctx:
+        consts = ctx.enter_context(tc.tile_pool(name="consts", bufs=1))
+        keep = ctx.enter_context(tc.tile_pool(name="keep", bufs=1))
+        raw = ctx.enter_context(tc.tile_pool(name="raw", bufs=2))
+        stage = ctx.enter_context(tc.tile_pool(name="stage", bufs=2))
+        psum = ctx.enter_context(tc.psum_pool(name="psum", bufs=1))
+
+        ident_f = consts.tile([P, P], F32, name="ident_f", tag="ident_f")
+        make_identity(nc, ident_f[:])
+        ident_b = consts.tile([P, P], BF16, name="ident_b", tag="ident_b")
+        make_identity(nc, ident_b[:])
+
+        wq = keep.tile([P, NC, NG, 512], U32, name="wq", tag="wq", align_bytes=64)
+        ws = keep.tile([P, NC, NG, 512], U8, name="ws", tag="ws", align_bytes=64)
+        dq = keep.tile([P, NT, NG, P], U32, name="dq", tag="dq", align_bytes=64)
+        ds = keep.tile([P, NT, NG, P], U8, name="ds", tag="ds", align_bytes=64)
+        lbT = keep.tile([P, NT, NC, 512], BF16, name="lbT", tag="lbT")
+        tT = keep.tile([P, NT, P], BF16, name="tT", tag="tT")
+
+        ctx.enter_context(tc.manual_schedule())
+
+        tiles = {}
+        state = {"next": 0}
+
+        def issue_load(ld):
+            kind = ld[0]
+            if kind == "w":
+                t = raw.tile([P, IN], BF16, name="wraw", tag="wraw", bufs=BUFS["w"])
+                row = 512 * ld[1] + P * ld[2]
+                nc.sync.dma_start(out=t[:], in_=W[row : row + P, :])
+            elif kind == "x":
+                t = raw.tile([P, IN], BF16, name="xraw", tag="xraw", bufs=BUFS["x"])
+                nc.sync.dma_start(out=t[:], in_=data[ld[1]])
+            elif kind == "l":
+                t = raw.tile([P, 2, 4, P], BF16, name="lraw", tag="lraw", bufs=BUFS["l"])
+                src = lora_b[ld[1]].rearrange("(j p i) r -> p j (i r)", j=NC, p=P, i=4)
+                nc.sync.dma_start(
+                    out=t[:].rearrange("p j i r -> p j (i r)"),
+                    in_=src[:, 2 * ld[2] : 2 * ld[2] + 2, :],
+                )
+            else:
+                t = raw.tile([P, NT, P], BF16, name="traw", tag="traw", bufs=BUFS["t"])
+                nc.sync.dma_start(out=t[:], in_=t_lora.rearrange("a g s r -> s (a g) r"))
+            tiles[ld] = t
+
+        def issue_ready_loads(r):
+            while state["next"] < len(order):
+                ld = order[state["next"]]
+                peers = by_kind[ld[0]]
+                n = peers.index(ld)
+                if n >= BUFS[ld[0]] and last_use[peers[n - BUFS[ld[0]]]] > r:
+                    break
+                issue_load(ld)
+                state["next"] += 1
+
+        def transposes(bu, k):
+            kind = bu[0]
+            if kind == "W" or kind == "D":
+                bank = psum.tile([P, 2, 2, P], F32, name="trf", tag="tr%d" % k)
+                for a in range(2):
+                    if kind == "W":
+                        words = tiles[("w", bu[1], 2 * bu[3] + a)][:].bitcast(F32)
+                        g = bu[2]
+                    else:
+                        words = tiles[("x", bu[1])][:].bitcast(F32)
+                        g = 2 * bu[2] + a
+                    for u in range(2):
+                        nc.tensor.transpose(
+                            bank[:, a, u, :], words[:, 256 * g + u : 256 * (g + 1) : 2], ident_f[:]
+                        )
+            elif kind == "L":
+                bank = psum.tile([P, 2, 4, P], BF16, name="trl", tag="tr%d" % k)
+                src = tiles[("l", bu[1], bu[2])]
+                for jj in range(2):
+                    for i in range(4):
+                        nc.tensor.transpose(bank[:, jj, i, :], src[:, jj, i, :], ident_b[:])
+            else:
+                bank = psum.tile([P, NT, P], BF16, name="trt", tag="tr%d" % k)
+                src = tiles[("t",)]
+                for m in range(NT):
+                    nc.tensor.transpose(bank[:, m, :], src[:, m, :], ident_b[:])
+            return bank
+
+        def copy_out(bu, bank, on_vector):
+            kind = bu[0]
+            if kind == "W" or kind == "D":
+                grp = stage.tile([P, 1024], BF16, name="grp", tag="grp", bufs=8, align_bytes=64)
+                dst = grp[:].bitcast(F32).rearrange("p (a r u) -> p a r u", a=2, u=2)
+                src = bank[:].rearrange("p a u r -> p a r u")
+                if on_vector:
+                    nc.vector.tensor_copy(out=dst, in_=src)
+                else:
+                    nc.scalar.copy(out=dst, in_=src)
+                return grp
+            if kind == "L":
+                nc.scalar.copy(
+                    out=lbT[:, bu[1], 2 * bu[2] : 2 * bu[2] + 2, :],
+                    in_=bank[:].rearrange("r j i p -> r j (i p)"),
+                )
+            else:
+                nc.scalar.copy(out=tT[:], in_=bank[:])
+            return None
+
+        def quantize(bu, grp):
+            if bu[0] == "W":
+                j, g, h = bu[1], bu[2], bu[3]
+                codes = wq[:, j, g, 256 * h : 256 * (h + 1)]
+                scales = ws[:, j, g, 256 * h : 256 * (h + 1)]
+            else:
+                m, gh = bu[1], bu[2]
+                codes = dq[:, m, 2 * gh : 2 * gh + 2, :].rearrange("p g r -> p (g r)")
+                scales = ds[:, m, 2 * gh : 2 * gh + 2, :].rearrange("p g r -> p (g r)")
+            nc.vector.quantize_mx(out=codes.bitcast(E5X4), scales=scales, in_=grp[:])
+
+        def matmuls(unit, n):
+            j, m = unit
+            pl = psum.tile([P, 512], F32, name="pl", tag="pl%d" % (n % 2))
+            nc.tensor.matmul(pl[:], lhsT=tT[:, m, :], rhs=lbT[:, m, j, :], start=True, stop=True)
+            delta = stage.tile([P, 512], F32, name="delta", tag="delta", bufs=3)
+            nc.scalar.activation(
+                out=delta[:].rearrange("s (p i) -> s p i", i=4),
+                in_=pl[:].rearrange("s (i p) -> s p i", i=4),
+                func=COPY,
+                scale=2.0,
+            )
+            acc = psum.tile([P, 512], F32, name="acc", tag="mx%d" % (n % 2))
+            for g in range(NG):
+                nc.tensor.matmul_mx(
+                    out=acc[:],
+                    lhsT=dq[:, m, g, :].bitcast(E5X4),
+                    lhsT_scale=ds[:, m, g, :],
+                    rhs=wq[:, j, g, :].bitcast(E5X4),
+                    rhs_scale=ws[:, j, g, :],
+                    start=(g == 0),
+                    stop=(g == NG - 1),
+                )
+            return acc, delta
+
+        def finish(unit, acc, delta):
+            j, m = unit
+            res = stage.tile([P, 512], F32, name="res", tag="res", bufs=4)
+            nc.vector.tensor_tensor(out=res[:], in0=acc[:], in1=delta[:], op=ADD)
+            nc.sync.dma_start(out=out[m, :, 512 * j : 512 * (j + 1)], in_=res[:])
+
+        issue_ready_loads(-1)
+        pending = []
+        n_units = 0
+        for r, (bus, units) in enumerate(rounds):
+            banks = [transposes(bu, k) for k, bu in enumerate(bus)]
+            for unit, acc, delta in pending:
+                finish(unit, acc, delta)
+            pending = []
+            grps = []
+            for k, bu in enumerate(bus):
+                if len(units) == 0:
+                    on_vector = k % 2 == 1 and bu[0] in ("W", "D")
+                else:
+                    on_vector = bu[0] == "D" and bu[2] == 0
+                grps.append((bu, copy_out(bu, banks[k], on_vector), on_vector))
+            for on_v in (False, True):
+                for bu, grp, on_vector in grps:
+                    if grp is not None and on_vector == on_v:
+                        quantize(bu, grp)
+            issue_ready_loads(r)
+            for unit in units:
+                acc, delta = matmuls(unit, n_units)
+                n_units += 1
+                pending.append((unit, acc, delta))
+                for old in pending[:-1]:
+                    finish(*old)
+                pending = pending[-1:]
+        for unit, acc, delta in pending:
+            finish(unit, acc, delta)

@@ -16,35 +16,70 @@ NT = 8
 NC = 4
 NG = 4
 IN = 2048
-OUT = 2048
 FLOPS = 2 * 1024 * 2048 * 2048 + 2 * 1024 * 2048 * 128
 
-BUFS = {"w": 10, "x": 4, "l": 6, "t": 1}
+BUFS = {"w": 6, "x": 4, "l": 6, "t": 1}
+DEI_BUFS = {"w": 6, "x": 4}
+WARM = 0
+DLEAD = 2
+HEAD = 1
+CAP = 4
+LEAD = 2
+DIRECT_ROUNDS = 0
+VSHARE = 0
+
+
+def needs_of(item):
+    j, m = item[1], item[2]
+    if item[0] == "PL":
+        return [("T",), ("L", m, j // 2)]
+    g = item[3]
+    return [("D", m, g // 2), ("W", j, g, 0), ("W", j, g, 1)]
 
 
 def build_rounds():
+    groups = []
+    for r in range(1, max(HEAD, NG) + 1):
+        groups.append(
+            [("MX", 0, m, g) for m in range(min(r, HEAD)) for g in range(min(r, NG)) if m == r - 1 or g == r - 1]
+        )
+    groups += [[("PL", 0, m)] for m in range(HEAD)]
+    for j in range(NC):
+        for m in range(NT):
+            if j > 0 or m >= HEAD:
+                groups.append([("PL", j, m)] + [("MX", j, m, g) for g in range(NG)])
+    need = {}
+    for n, grp in enumerate(groups):
+        for item in grp:
+            for bu in needs_of(item):
+                if bu not in need:
+                    need[bu] = n
+    slots = [[] for n in groups]
+    left = sorted(need, key=lambda bu: need[bu])
+    held = []
+    for n in reversed(range(len(groups))):
+        while left and need[left[-1]] - LEAD >= n:
+            held = [left[-1]] + held
+            left = left[:-1]
+        if len(held) >= CAP:
+            slots[n] = held[-CAP:]
+            held = held[:-CAP]
+    left += held
     rounds = []
-    rounds.append(([("W", 0, g, 0) for g in range(NG)], []))
-    rounds.append(([("W", 0, g, 1) for g in range(NG)], []))
-    rounds.append(([("D", 0, 0), ("D", 0, 1), ("T",), ("L", 0, 0)], []))
-    for m in range(NT):
-        bus = []
-        if m + 1 < NT:
-            bus += [("D", m + 1, 0), ("D", m + 1, 1), ("L", m + 1, 0)]
-        bus.append(("W", 1, m % NG, m // NG))
-        rounds.append((bus, [(0, m)]))
-    for q in range(4):
-        bus = [("W", 2, (2 * q) % NG, (2 * q) // NG), ("W", 2, (2 * q + 1) % NG, (2 * q + 1) // NG)]
-        bus += [("L", 2 * q, 1), ("L", 2 * q + 1, 1)]
-        rounds.append((bus, [(1, 2 * q), (1, 2 * q + 1)]))
-    for q in range(4):
-        bus = [("W", 3, (2 * q) % NG, (2 * q) // NG), ("W", 3, (2 * q + 1) % NG, (2 * q + 1) // NG)]
-        rounds.append((bus, [(2, 2 * q), (2, 2 * q + 1)]))
-    rounds.append(([], [(3, m) for m in range(NT)]))
+    while left:
+        rounds.append([left[:CAP], []])
+        left = left[CAP:]
+    for n, grp in enumerate(groups):
+        if slots[n] or not rounds:
+            rounds.append([slots[n], [grp]])
+        else:
+            rounds[-1][1].append(grp)
     return rounds
 
 
 def loads_of(bu):
+    if bu[0] == "W" and bu[1] == 0:
+        return [("w", 0, bu[2])]
     if bu[0] == "W":
         return [("w", bu[1], 2 * bu[3]), ("w", bu[1], 2 * bu[3] + 1)]
     if bu[0] == "D":
@@ -59,12 +94,14 @@ def tile_linear_pa_kernel(tc, data, W, t_lora, lora_b, out):
     rounds = build_rounds()
 
     order = []
+    first_use = {}
     last_use = {}
-    for r, (bus, units) in enumerate(rounds):
+    for r, (bus, groups) in enumerate(rounds):
         for bu in bus:
             for ld in loads_of(bu):
                 if ld not in last_use:
                     order.append(ld)
+                    first_use[ld] = r
                 last_use[ld] = r
     by_kind = {"w": [], "x": [], "l": [], "t": []}
     for ld in order:
@@ -92,11 +129,24 @@ def tile_linear_pa_kernel(tc, data, W, t_lora, lora_b, out):
         ctx.enter_context(tc.manual_schedule())
 
         tiles = {}
-        state = {"next": 0}
+        sorted_words = {}
+        state = {"next_load": 0, "next_sort": 0, "drains": 0}
+        free_banks = list(range(8))
+
+        def take_bank(shape, dtype, name):
+            b = free_banks[0]
+            free_banks.remove(b)
+            return b, psum.tile(shape, dtype, name=name, tag="bank%d" % b)
 
         def issue_load(ld):
             kind = ld[0]
-            if kind == "w":
+            if kind == "w" and ld[1] == 0:
+                t = raw.tile([P, IN], BF16, name="wraw", tag="wraw", bufs=BUFS["w"])
+                nc.sync.dma_start(
+                    out=t[:].rearrange("p (i k) -> p i k", i=4),
+                    in_=W[0:512, 512 * ld[2] : 512 * (ld[2] + 1)].rearrange("(i p) k -> p i k", p=P),
+                )
+            elif kind == "w":
                 t = raw.tile([P, IN], BF16, name="wraw", tag="wraw", bufs=BUFS["w"])
                 row = 512 * ld[1] + P * ld[2]
                 nc.sync.dma_start(out=t[:], in_=W[row : row + P, :])
@@ -115,63 +165,97 @@ def tile_linear_pa_kernel(tc, data, W, t_lora, lora_b, out):
                 nc.sync.dma_start(out=t[:], in_=t_lora.rearrange("a g s r -> s (a g) r"))
             tiles[ld] = t
 
+        def is_direct(ld):
+            return first_use[ld] < DIRECT_ROUNDS
+
+        def released(ld, r):
+            if ld[0] in DEI_BUFS and not is_direct(ld):
+                return ld in sorted_words
+            return last_use[ld] <= r
+
         def issue_ready_loads(r):
-            while state["next"] < len(order):
-                ld = order[state["next"]]
+            while state["next_load"] < len(order):
+                ld = order[state["next_load"]]
                 peers = by_kind[ld[0]]
                 n = peers.index(ld)
-                if n >= BUFS[ld[0]] and last_use[peers[n - BUFS[ld[0]]]] > r:
+                if n >= BUFS[ld[0]] and not released(peers[n - BUFS[ld[0]]], r):
                     break
                 issue_load(ld)
-                state["next"] += 1
+                state["next_load"] += 1
 
-        def transposes(bu, k):
+        word_loads = [ld for ld in order if ld[0] in DEI_BUFS and not is_direct(ld)]
+
+        def sort_words(r):
+            while state["next_sort"] < len(word_loads):
+                ld = word_loads[state["next_sort"]]
+                if first_use[ld] > r + DLEAD or ld not in tiles:
+                    break
+                peers = [x for x in word_loads if x[0] == ld[0]]
+                n = peers.index(ld)
+                if n >= DEI_BUFS[ld[0]] and last_use[peers[n - DEI_BUFS[ld[0]]]] > r:
+                    break
+                dei = stage.tile([P, NG, 2, P], F32, name="dei" + ld[0], tag="dei" + ld[0], bufs=DEI_BUFS[ld[0]])
+                nc.vector.tensor_copy(
+                    out=dei[:],
+                    in_=tiles[ld][:].bitcast(F32).rearrange("r (g p u) -> r g u p", g=NG, u=2),
+                )
+                sorted_words[ld] = dei
+                state["next_sort"] += 1
+
+        def words_of(ld, n, u):
+            if is_direct(ld):
+                return tiles[ld][:].bitcast(F32)[:, 256 * n + u : 256 * (n + 1) : 2]
+            return sorted_words[ld][:, n, u, :]
+
+        def transposes(bu):
             kind = bu[0]
             if kind == "W" or kind == "D":
-                bank = psum.tile([P, 2, 2, P], F32, name="trf", tag="tr%d" % k)
+                b, bank = take_bank([P, 2, 2, P], F32, "trf")
                 for a in range(2):
-                    if kind == "W":
-                        words = tiles[("w", bu[1], 2 * bu[3] + a)][:].bitcast(F32)
-                        g = bu[2]
+                    if kind == "W" and bu[1] == 0:
+                        ld, n = ("w", 0, bu[2]), 2 * bu[3] + a
+                    elif kind == "W":
+                        ld, n = ("w", bu[1], 2 * bu[3] + a), bu[2]
                     else:
-                        words = tiles[("x", bu[1])][:].bitcast(F32)
-                        g = 2 * bu[2] + a
+                        ld, n = ("x", bu[1]), 2 * bu[2] + a
                     for u in range(2):
-                        nc.tensor.transpose(
-                            bank[:, a, u, :], words[:, 256 * g + u : 256 * (g + 1) : 2], ident_f[:]
-                        )
+                        nc.tensor.transpose(bank[:, a, u, :], words_of(ld, n, u), ident_f[:])
             elif kind == "L":
-                bank = psum.tile([P, 2, 4, P], BF16, name="trl", tag="tr%d" % k)
+                b, bank = take_bank([P, 2, 4, P], BF16, "trl")
                 src = tiles[("l", bu[1], bu[2])]
                 for jj in range(2):
                     for i in range(4):
                         nc.tensor.transpose(bank[:, jj, i, :], src[:, jj, i, :], ident_b[:])
             else:
-                bank = psum.tile([P, NT, P], BF16, name="trt", tag="tr%d" % k)
+                b, bank = take_bank([P, NT, P], BF16, "trt")
                 src = tiles[("t",)]
                 for m in range(NT):
                     nc.tensor.transpose(bank[:, m, :], src[:, m, :], ident_b[:])
-            return bank
+            return b, bank
 
-        def copy_out(bu, bank, on_vector):
+        def copy_out(bu, b, bank):
             kind = bu[0]
+            grp = None
+            on_vector = False
             if kind == "W" or kind == "D":
                 grp = stage.tile([P, 1024], BF16, name="grp", tag="grp", bufs=8, align_bytes=64)
                 dst = grp[:].bitcast(F32).rearrange("p (a r u) -> p a r u", a=2, u=2)
                 src = bank[:].rearrange("p a u r -> p a r u")
+                state["drains"] += 1
+                on_vector = VSHARE > 0 and state["drains"] % VSHARE == 0
                 if on_vector:
                     nc.vector.tensor_copy(out=dst, in_=src)
                 else:
                     nc.scalar.copy(out=dst, in_=src)
-                return grp
-            if kind == "L":
+            elif kind == "L":
                 nc.scalar.copy(
                     out=lbT[:, bu[1], 2 * bu[2] : 2 * bu[2] + 2, :],
                     in_=bank[:].rearrange("r j i p -> r j (i p)"),
                 )
             else:
                 nc.scalar.copy(out=tT[:], in_=bank[:])
-            return None
+            free_banks.append(b)
+            return bu, grp, on_vector
 
         def quantize(bu, grp):
             if bu[0] == "W":
@@ -184,21 +268,29 @@ def tile_linear_pa_kernel(tc, data, W, t_lora, lora_b, out):
                 scales = ds[:, m, 2 * gh : 2 * gh + 2, :].rearrange("p g r -> p (g r)")
             nc.vector.quantize_mx(out=codes.bitcast(E5X4), scales=scales, in_=grp[:])
 
-        def matmuls(unit, n):
-            j, m = unit
-            pl = psum.tile([P, 512], F32, name="pl", tag="pl%d" % (n % 2))
-            nc.tensor.matmul(pl[:], lhsT=tT[:, m, :], rhs=lbT[:, m, j, :], start=True, stop=True)
-            delta = stage.tile([P, 512], F32, name="delta", tag="delta", bufs=3)
-            nc.scalar.activation(
-                out=delta[:].rearrange("s (p i) -> s p i", i=4),
-                in_=pl[:].rearrange("s (i p) -> s p i", i=4),
-                func=COPY,
-                scale=2.0,
-            )
-            acc = psum.tile([P, 512], F32, name="acc", tag="mx%d" % (n % 2))
-            for g in range(NG):
+        accs = {}
+        deltas = {}
+
+        def matmul_item(item):
+            j, m = item[1], item[2]
+            if item[0] == "PL":
+                bp, pl = take_bank([P, 512], F32, "pl")
+                nc.tensor.matmul(pl[:], lhsT=tT[:, m, :], rhs=lbT[:, m, j, :], start=True, stop=True)
+                delta = stage.tile([P, 512], F32, name="delta", tag="delta", bufs=4)
+                nc.scalar.activation(
+                    out=delta[:].rearrange("s (p i) -> s p i", i=4),
+                    in_=pl[:].rearrange("s (i p) -> s p i", i=4),
+                    func=COPY,
+                    scale=2.0,
+                )
+                free_banks.append(bp)
+                deltas[(j, m)] = delta
+            else:
+                g = item[3]
+                if g == 0:
+                    accs[(j, m)] = take_bank([P, 512], F32, "acc")
                 nc.tensor.matmul_mx(
-                    out=acc[:],
+                    out=accs[(j, m)][1][:],
                     lhsT=dq[:, m, g, :].bitcast(E5X4),
                     lhsT_scale=ds[:, m, g, :],
                     rhs=wq[:, j, g, :].bitcast(E5X4),
@@ -206,40 +298,51 @@ def tile_linear_pa_kernel(tc, data, W, t_lora, lora_b, out):
                     start=(g == 0),
                     stop=(g == NG - 1),
                 )
-            return acc, delta
 
-        def finish(unit, acc, delta):
+        def finish(unit):
             j, m = unit
+            ba, acc = accs[unit]
             res = stage.tile([P, 512], F32, name="res", tag="res", bufs=4)
-            nc.vector.tensor_tensor(out=res[:], in0=acc[:], in1=delta[:], op=ADD)
+            nc.vector.tensor_tensor(out=res[:], in0=acc[:], in1=deltas[unit][:], op=ADD)
+            free_banks.append(ba)
             nc.sync.dma_start(out=out[m, :, 512 * j : 512 * (j + 1)], in_=res[:])
 
         issue_ready_loads(-1)
+        if WARM:
+            zeros = consts.tile([P, 512], BF16, name="zeros", tag="zeros")
+            nc.vector.memset(zeros[:], 0.0)
+            bw, warm = take_bank([P, 512], F32, "warm")
+            for n in range(WARM):
+                nc.tensor.matmul(warm[:], lhsT=zeros[:, 0:P], rhs=zeros[:], start=True, stop=True)
+            free_banks.append(bw)
+        sort_words(-1)
+        issue_ready_loads(-1)
         pending = []
-        n_units = 0
-        for r, (bus, units) in enumerate(rounds):
-            banks = [transposes(bu, k) for k, bu in enumerate(bus)]
-            for unit, acc, delta in pending:
-                finish(unit, acc, delta)
+        closed = set()
+        for r, (bus, groups) in enumerate(rounds):
+            banks = [transposes(bu) for bu in bus]
+            for unit in pending:
+                finish(unit)
             pending = []
-            grps = []
-            for k, bu in enumerate(bus):
-                if len(units) == 0:
-                    on_vector = k % 2 == 1 and bu[0] in ("W", "D")
-                else:
-                    on_vector = bu[0] == "D" and bu[2] == 0
-                grps.append((bu, copy_out(bu, banks[k], on_vector), on_vector))
+            drained = [copy_out(bu, banks[k][0], banks[k][1]) for k, bu in enumerate(bus)]
             for on_v in (False, True):
-                for bu, grp, on_vector in grps:
+                for bu, grp, on_vector in drained:
                     if grp is not None and on_vector == on_v:
                         quantize(bu, grp)
+            sort_words(r)
             issue_ready_loads(r)
-            for unit in units:
-                acc, delta = matmuls(unit, n_units)
-                n_units += 1
-                pending.append((unit, acc, delta))
-                for old in pending[:-1]:
-                    finish(*old)
-                pending = pending[-1:]
-        for unit, acc, delta in pending:
-            finish(unit, acc, delta)
+            for grp in groups:
+                for item in grp:
+                    matmul_item(item)
+                    if item[0] == "MX" and item[3] == NG - 1:
+                        closed.add((item[1], item[2]))
+                for unit in pending:
+                    finish(unit)
+                pending = []
+                for item in grp:
+                    unit = (item[1], item[2])
+                    if unit in closed and unit in deltas and unit not in pending:
+                        pending.append(unit)
+                        closed.remove(unit)
+        for unit in pending:
+            finish(unit)

@@ -20,13 +20,17 @@ FLOPS = 2 * 1024 * 2048 * 2048 + 2 * 1024 * 2048 * 128
 
 BUFS = {"w": 6, "x": 4, "l": 6, "t": 1}
 DEI_BUFS = {"w": 6, "x": 4}
-WARM = 0
+WARM = 8
 DLEAD = 2
 HEAD = 1
 CAP = 4
 LEAD = 2
-DIRECT_ROUNDS = 0
-VSHARE = 0
+DIRECT_ROUNDS = 5
+VEVERY = 6
+VORDER_FROM = 99
+SANDWICH = 1
+SPREAD = 0
+TAIL_PARTS = 2
 
 
 def needs_of(item):
@@ -53,7 +57,9 @@ def build_rounds():
         for item in grp:
             for bu in needs_of(item):
                 if bu not in need:
-                    need[bu] = n
+                    need[bu] = n - SANDWICH if item[0] == "PL" else n
+                    if bu[0] == "W" and bu[1] == 1:
+                        need[bu] = n - SPREAD * (7 - 2 * bu[2] - bu[3])
     slots = [[] for n in groups]
     left = sorted(need, key=lambda bu: need[bu])
     held = []
@@ -74,6 +80,13 @@ def build_rounds():
             rounds.append([slots[n], [grp]])
         else:
             rounds[-1][1].append(grp)
+    if SANDWICH:
+        for r in range(1, len(rounds)):
+            bus, grps = rounds[r]
+            if bus and grps and grps[0][0][0] == "PL" and rounds[r - 1][1]:
+                first = grps[0][0]
+                grps[0] = [("PLb", first[1], first[2])] + grps[0][1:]
+                rounds[r - 1][1].append([("PLa", first[1], first[2])])
     return rounds
 
 
@@ -233,16 +246,11 @@ def tile_linear_pa_kernel(tc, data, W, t_lora, lora_b, out):
                     nc.tensor.transpose(bank[:, m, :], src[:, m, :], ident_b[:])
             return b, bank
 
-        def copy_out(bu, b, bank):
+        def copy_out(bu, b, bank, grp, half, on_vector):
             kind = bu[0]
-            grp = None
-            on_vector = False
             if kind == "W" or kind == "D":
-                grp = stage.tile([P, 1024], BF16, name="grp", tag="grp", bufs=8, align_bytes=64)
-                dst = grp[:].bitcast(F32).rearrange("p (a r u) -> p a r u", a=2, u=2)
+                dst = grp[:, 1024 * half : 1024 * (half + 1)].bitcast(F32).rearrange("p (a r u) -> p a r u", a=2, u=2)
                 src = bank[:].rearrange("p a u r -> p a r u")
-                state["drains"] += 1
-                on_vector = VSHARE > 0 and state["drains"] % VSHARE == 0
                 if on_vector:
                     nc.vector.tensor_copy(out=dst, in_=src)
                 else:
@@ -255,27 +263,32 @@ def tile_linear_pa_kernel(tc, data, W, t_lora, lora_b, out):
             else:
                 nc.scalar.copy(out=tT[:], in_=bank[:])
             free_banks.append(b)
-            return bu, grp, on_vector
 
-        def quantize(bu, grp):
-            if bu[0] == "W":
-                j, g, h = bu[1], bu[2], bu[3]
-                codes = wq[:, j, g, 256 * h : 256 * (h + 1)]
-                scales = ws[:, j, g, 256 * h : 256 * (h + 1)]
+        def quantize(key, halves, grp):
+            lo, hi = 256 * halves[0], 256 * (halves[-1] + 1)
+            if key[0] == "W":
+                codes = wq[:, key[1], key[2], lo:hi]
+                scales = ws[:, key[1], key[2], lo:hi]
             else:
-                m, gh = bu[1], bu[2]
-                codes = dq[:, m, 2 * gh : 2 * gh + 2, :].rearrange("p g r -> p (g r)")
-                scales = ds[:, m, 2 * gh : 2 * gh + 2, :].rearrange("p g r -> p (g r)")
-            nc.vector.quantize_mx(out=codes.bitcast(E5X4), scales=scales, in_=grp[:])
+                codes = dq[:, key[1], :, :].rearrange("p g r -> p (g r)")[:, lo:hi]
+                scales = ds[:, key[1], :, :].rearrange("p g r -> p (g r)")[:, lo:hi]
+            nc.vector.quantize_mx(out=codes.bitcast(E5X4), scales=scales, in_=grp[:, 4 * lo : 4 * hi])
 
         accs = {}
+        pls = {}
         deltas = {}
 
         def matmul_item(item):
             j, m = item[1], item[2]
-            if item[0] == "PL":
-                bp, pl = take_bank([P, 512], F32, "pl")
-                nc.tensor.matmul(pl[:], lhsT=tT[:, m, :], rhs=lbT[:, m, j, :], start=True, stop=True)
+            if item[0] in ("PL", "PLa", "PLb"):
+                if item[0] != "PLb":
+                    pls[(j, m)] = take_bank([P, 512], F32, "pl")
+                bp, pl = pls[(j, m)]
+                lo = 256 if item[0] == "PLb" else 0
+                hi = 256 if item[0] == "PLa" else 512
+                nc.tensor.matmul(pl[:, lo:hi], lhsT=tT[:, m, :], rhs=lbT[:, m, j, lo:hi], start=True, stop=True)
+                if item[0] == "PLa":
+                    return
                 delta = stage.tile([P, 512], F32, name="delta", tag="delta", bufs=4)
                 nc.scalar.activation(
                     out=delta[:].rearrange("s (p i) -> s p i", i=4),
@@ -299,13 +312,15 @@ def tile_linear_pa_kernel(tc, data, W, t_lora, lora_b, out):
                     stop=(g == NG - 1),
                 )
 
-        def finish(unit):
+        def finish(unit, parts=1):
             j, m = unit
             ba, acc = accs[unit]
-            res = stage.tile([P, 512], F32, name="res", tag="res", bufs=4)
-            nc.vector.tensor_tensor(out=res[:], in0=acc[:], in1=deltas[unit][:], op=ADD)
+            width = 512 // parts
+            for c in range(0, 512, width):
+                res = stage.tile([P, width], F32, name="res", tag="res", bufs=4)
+                nc.vector.tensor_tensor(out=res[:], in0=acc[:, c : c + width], in1=deltas[unit][:, c : c + width], op=ADD)
+                nc.sync.dma_start(out=out[m, :, 512 * j + c : 512 * j + c + width], in_=res[:])
             free_banks.append(ba)
-            nc.sync.dma_start(out=out[m, :, 512 * j : 512 * (j + 1)], in_=res[:])
 
         issue_ready_loads(-1)
         if WARM:
@@ -324,13 +339,31 @@ def tile_linear_pa_kernel(tc, data, W, t_lora, lora_b, out):
             for unit in pending:
                 finish(unit)
             pending = []
-            drained = [copy_out(bu, banks[k][0], banks[k][1]) for k, bu in enumerate(bus)]
+            if r >= VORDER_FROM:
+                sort_words(r)
+                issue_ready_loads(r)
+            pairs = {}
+            for k, bu in enumerate(bus):
+                grp, half, on_vector = None, 0, False
+                if bu[0] in ("W", "D"):
+                    key = bu[:-1]
+                    half = bu[-1]
+                    if key not in pairs:
+                        new = stage.tile([P, 2048], BF16, name="grp", tag="grp", bufs=5, align_bytes=64)
+                        pairs[key] = [new, [], False]
+                    grp = pairs[key][0]
+                    state["drains"] += 1
+                    on_vector = VEVERY > 0 and state["drains"] % VEVERY == 0
+                    pairs[key][1].append(half)
+                    pairs[key][2] = pairs[key][2] or on_vector
+                copy_out(bu, banks[k][0], banks[k][1], grp, half, on_vector)
             for on_v in (False, True):
-                for bu, grp, on_vector in drained:
-                    if grp is not None and on_vector == on_v:
-                        quantize(bu, grp)
-            sort_words(r)
-            issue_ready_loads(r)
+                for key in pairs:
+                    if pairs[key][2] == on_v:
+                        quantize(key, pairs[key][1], pairs[key][0])
+            if r < VORDER_FROM:
+                sort_words(r)
+                issue_ready_loads(r)
             for grp in groups:
                 for item in grp:
                     matmul_item(item)
@@ -345,4 +378,4 @@ def tile_linear_pa_kernel(tc, data, W, t_lora, lora_b, out):
                         pending.append(unit)
                         closed.remove(unit)
         for unit in pending:
-            finish(unit)
+            finish(unit, TAIL_PARTS)

@@ -18,76 +18,45 @@ NG = 4
 IN = 2048
 FLOPS = 2 * 1024 * 2048 * 2048 + 2 * 1024 * 2048 * 128
 
-BUFS = {"w": 6, "x": 4, "l": 6, "t": 1}
-DEI_BUFS = {"w": 6, "x": 4}
+BUFS = {"raw": 8, "lraw": 8, "traw": 1}
+DEI_BUFS = 8
+RES_BUFS = 10
+GRP_BUFS = 6
 WARM = 8
-DLEAD = 2
-HEAD = 1
-CAP = 4
-LEAD = 2
-DIRECT_ROUNDS = 5
-VEVERY = 6
-VORDER_FROM = 99
-SANDWICH = 1
-SPREAD = 0
+VEVERY = 4
+LAG = 1
+AHEAD = 4
+PRESORT = 9
+CUTS = [0, 1, 4, 7, 14, 22, 32]
+HOLD = 2
 TAIL_PARTS = 2
 
 
-def needs_of(item):
-    j, m = item[1], item[2]
-    if item[0] == "PL":
-        return [("T",), ("L", m, j // 2)]
-    g = item[3]
-    return [("D", m, g // 2), ("W", j, g, 0), ("W", j, g, 1)]
+def w_banks(j):
+    if j == 0:
+        return [("W", j, g, h) for g in range(NG) for h in range(2)]
+    return [("W", j, g, h) for h in range(2) for g in range(NG)]
 
 
-def build_rounds():
-    groups = []
-    for r in range(1, max(HEAD, NG) + 1):
-        groups.append(
-            [("MX", 0, m, g) for m in range(min(r, HEAD)) for g in range(min(r, NG)) if m == r - 1 or g == r - 1]
-        )
-    groups += [[("PL", 0, m)] for m in range(HEAD)]
-    for j in range(NC):
-        for m in range(NT):
-            if j > 0 or m >= HEAD:
-                groups.append([("PL", j, m)] + [("MX", j, m, g) for g in range(NG)])
-    need = {}
-    for n, grp in enumerate(groups):
-        for item in grp:
-            for bu in needs_of(item):
-                if bu not in need:
-                    need[bu] = n - SANDWICH if item[0] == "PL" else n
-                    if bu[0] == "W" and bu[1] == 1:
-                        need[bu] = n - SPREAD * (7 - 2 * bu[2] - bu[3])
-    slots = [[] for n in groups]
-    left = sorted(need, key=lambda bu: need[bu])
-    held = []
-    for n in reversed(range(len(groups))):
-        while left and need[left[-1]] - LEAD >= n:
-            held = [left[-1]] + held
-            left = left[:-1]
-        if len(held) >= CAP:
-            slots[n] = held[-CAP:]
-            held = held[:-CAP]
-    left += held
-    rounds = []
-    while left:
-        rounds.append([left[:CAP], []])
-        left = left[CAP:]
-    for n, grp in enumerate(groups):
-        if slots[n] or not rounds:
-            rounds.append([slots[n], [grp]])
-        else:
-            rounds[-1][1].append(grp)
-    if SANDWICH:
-        for r in range(1, len(rounds)):
-            bus, grps = rounds[r]
-            if bus and grps and grps[0][0][0] == "PL" and rounds[r - 1][1]:
-                first = grps[0][0]
-                grps[0] = [("PLb", first[1], first[2])] + grps[0][1:]
-                rounds[r - 1][1].append([("PLa", first[1], first[2])])
-    return rounds
+def token_banks(m):
+    return [("L", m, 0), ("D", m, 0), ("D", m, 1)]
+
+
+def build_phases():
+    units = [(j, m) for j in range(NC) for m in range(NT)]
+    runs = [
+        [("D", 0, 0), ("D", 0, 1)] + w_banks(0) + [("T",), ("L", 0, 0)] + token_banks(1),
+        token_banks(2) + token_banks(3) + token_banks(4),
+        token_banks(5) + token_banks(6) + token_banks(7),
+        w_banks(1),
+        w_banks(2) + [("L", m, 1) for m in range(NT)],
+        w_banks(3),
+    ]
+    phases = []
+    for n, run in enumerate(runs):
+        phases.append(("run", run))
+        phases.append(("block", units[CUTS[n] : CUTS[n + 1]]))
+    return phases
 
 
 def loads_of(bu):
@@ -102,23 +71,32 @@ def loads_of(bu):
     return [("t",)]
 
 
+def tag_of(ld):
+    return {"w": "raw", "x": "raw", "l": "lraw", "t": "traw"}[ld[0]]
+
+
+def is_direct(ld):
+    return ld[0] == "w" and ld[1] == 0 or ld[0] == "x" and ld[1] < 2
+
+
 def tile_linear_pa_kernel(tc, data, W, t_lora, lora_b, out):
     nc = tc.nc
-    rounds = build_rounds()
+    phases = build_phases()
 
+    seq = [bu for kind, items in phases if kind == "run" for bu in items]
     order = []
     first_use = {}
     last_use = {}
-    for r, (bus, groups) in enumerate(rounds):
-        for bu in bus:
-            for ld in loads_of(bu):
-                if ld not in last_use:
-                    order.append(ld)
-                    first_use[ld] = r
-                last_use[ld] = r
-    by_kind = {"w": [], "x": [], "l": [], "t": []}
+    for n, bu in enumerate(seq):
+        for ld in loads_of(bu):
+            if ld not in last_use:
+                order.append(ld)
+                first_use[ld] = n
+            last_use[ld] = n
+    by_tag = {"raw": [], "lraw": [], "traw": []}
     for ld in order:
-        by_kind[ld[0]].append(ld)
+        by_tag[tag_of(ld)].append(ld)
+    word_loads = [ld for ld in order if tag_of(ld) == "raw" and not is_direct(ld)]
 
     with ExitStack() as ctx:
         consts = ctx.enter_context(tc.tile_pool(name="consts", bufs=1))
@@ -143,7 +121,7 @@ def tile_linear_pa_kernel(tc, data, W, t_lora, lora_b, out):
 
         tiles = {}
         sorted_words = {}
-        state = {"next_load": 0, "next_sort": 0, "drains": 0}
+        state = {"next_load": 0, "next_sort": 0, "banks": 0, "drains": 0}
         free_banks = list(range(8))
 
         def take_bank(shape, dtype, name):
@@ -154,66 +132,65 @@ def tile_linear_pa_kernel(tc, data, W, t_lora, lora_b, out):
         def issue_load(ld):
             kind = ld[0]
             if kind == "w" and ld[1] == 0:
-                t = raw.tile([P, IN], BF16, name="wraw", tag="wraw", bufs=BUFS["w"])
+                t = raw.tile([P, IN], BF16, name="raw", tag="raw", bufs=BUFS["raw"])
                 nc.sync.dma_start(
                     out=t[:].rearrange("p (i k) -> p i k", i=4),
                     in_=W[0:512, 512 * ld[2] : 512 * (ld[2] + 1)].rearrange("(i p) k -> p i k", p=P),
                 )
             elif kind == "w":
-                t = raw.tile([P, IN], BF16, name="wraw", tag="wraw", bufs=BUFS["w"])
+                t = raw.tile([P, IN], BF16, name="raw", tag="raw", bufs=BUFS["raw"])
                 row = 512 * ld[1] + P * ld[2]
                 nc.sync.dma_start(out=t[:], in_=W[row : row + P, :])
             elif kind == "x":
-                t = raw.tile([P, IN], BF16, name="xraw", tag="xraw", bufs=BUFS["x"])
+                t = raw.tile([P, IN], BF16, name="raw", tag="raw", bufs=BUFS["raw"])
                 nc.sync.dma_start(out=t[:], in_=data[ld[1]])
             elif kind == "l":
-                t = raw.tile([P, 2, 4, P], BF16, name="lraw", tag="lraw", bufs=BUFS["l"])
+                t = raw.tile([P, 2, 4, P], BF16, name="lraw", tag="lraw", bufs=BUFS["lraw"])
                 src = lora_b[ld[1]].rearrange("(j p i) r -> p j (i r)", j=NC, p=P, i=4)
                 nc.sync.dma_start(
                     out=t[:].rearrange("p j i r -> p j (i r)"),
                     in_=src[:, 2 * ld[2] : 2 * ld[2] + 2, :],
                 )
             else:
-                t = raw.tile([P, NT, P], BF16, name="traw", tag="traw", bufs=BUFS["t"])
+                t = raw.tile([P, NT, P], BF16, name="traw", tag="traw", bufs=BUFS["traw"])
                 nc.sync.dma_start(out=t[:], in_=t_lora.rearrange("a g s r -> s (a g) r"))
             tiles[ld] = t
 
-        def is_direct(ld):
-            return first_use[ld] < DIRECT_ROUNDS
-
-        def released(ld, r):
-            if ld[0] in DEI_BUFS and not is_direct(ld):
+        def released(ld):
+            if ld in word_loads:
                 return ld in sorted_words
-            return last_use[ld] <= r
+            return last_use[ld] < state["banks"]
 
-        def issue_ready_loads(r):
+        def issue_ready_loads():
             while state["next_load"] < len(order):
                 ld = order[state["next_load"]]
-                peers = by_kind[ld[0]]
+                peers = by_tag[tag_of(ld)]
                 n = peers.index(ld)
-                if n >= BUFS[ld[0]] and not released(peers[n - BUFS[ld[0]]], r):
+                depth = BUFS[tag_of(ld)]
+                if n >= depth and not released(peers[n - depth]):
                     break
                 issue_load(ld)
                 state["next_load"] += 1
 
-        word_loads = [ld for ld in order if ld[0] in DEI_BUFS and not is_direct(ld)]
+        def unsorted_before(limit):
+            return [ld for ld in word_loads[state["next_sort"] :] if first_use[ld] < limit]
 
-        def sort_words(r):
-            while state["next_sort"] < len(word_loads):
-                ld = word_loads[state["next_sort"]]
-                if first_use[ld] > r + DLEAD or ld not in tiles:
+        def sort_words(count):
+            for c in range(count):
+                n = state["next_sort"]
+                if n >= len(word_loads) or word_loads[n] not in tiles:
                     break
-                peers = [x for x in word_loads if x[0] == ld[0]]
-                n = peers.index(ld)
-                if n >= DEI_BUFS[ld[0]] and last_use[peers[n - DEI_BUFS[ld[0]]]] > r:
+                if n >= DEI_BUFS and last_use[word_loads[n - DEI_BUFS]] >= state["banks"]:
                     break
-                dei = stage.tile([P, NG, 2, P], F32, name="dei" + ld[0], tag="dei" + ld[0], bufs=DEI_BUFS[ld[0]])
+                ld = word_loads[n]
+                dei = stage.tile([P, NG, 2, P], F32, name="dei", tag="dei", bufs=DEI_BUFS)
                 nc.vector.tensor_copy(
                     out=dei[:],
                     in_=tiles[ld][:].bitcast(F32).rearrange("r (g p u) -> r g u p", g=NG, u=2),
                 )
                 sorted_words[ld] = dei
                 state["next_sort"] += 1
+            issue_ready_loads()
 
         def words_of(ld, n, u):
             if is_direct(ld):
@@ -244,17 +221,52 @@ def tile_linear_pa_kernel(tc, data, W, t_lora, lora_b, out):
                 src = tiles[("t",)]
                 for m in range(NT):
                     nc.tensor.transpose(bank[:, m, :], src[:, m, :], ident_b[:])
+            state["banks"] += 1
             return b, bank
 
-        def copy_out(bu, b, bank, grp, half, on_vector):
+        pairs = {}
+        full_pairs = []
+
+        def quantize(key):
+            grp = pairs[key]
+            if key[0] == "W" and len(key) == 4:
+                lo = 256 * key[3]
+                codes = wq[:, key[1], key[2], lo : lo + 256]
+                scales = ws[:, key[1], key[2], lo : lo + 256]
+            elif key[0] == "W":
+                codes = wq[:, key[1], key[2], :]
+                scales = ws[:, key[1], key[2], :]
+            else:
+                codes = dq[:, key[1], :, :].rearrange("p g r -> p (g r)")
+                scales = ds[:, key[1], :, :].rearrange("p g r -> p (g r)")
+            nc.vector.quantize_mx(out=codes.bitcast(E5X4), scales=scales, in_=grp[:])
+
+        def quantize_but(keep_back):
+            while len(full_pairs) > keep_back:
+                quantize(full_pairs[0])
+                full_pairs.remove(full_pairs[0])
+
+        def drain(entry):
+            bu, b, bank = entry
             kind = bu[0]
             if kind == "W" or kind == "D":
+                alone = kind == "W" and bu[1] > 0
+                key = bu if alone else bu[:-1]
+                half = 0 if alone else bu[-1]
+                if half == 0:
+                    width = 1024 if alone else 2048
+                    pairs[key] = stage.tile([P, width], BF16, name="grp", tag="grp", bufs=GRP_BUFS, align_bytes=64)
+                grp = pairs[key]
                 dst = grp[:, 1024 * half : 1024 * (half + 1)].bitcast(F32).rearrange("p (a r u) -> p a r u", a=2, u=2)
                 src = bank[:].rearrange("p a u r -> p a r u")
-                if on_vector:
+                state["drains"] += 1
+                if state["drains"] % VEVERY == 0:
                     nc.vector.tensor_copy(out=dst, in_=src)
                 else:
                     nc.scalar.copy(out=dst, in_=src)
+                if half == 1 or alone:
+                    full_pairs.append(key)
+                    quantize_but(1)
             elif kind == "L":
                 nc.scalar.copy(
                     out=lbT[:, bu[1], 2 * bu[2] : 2 * bu[2] + 2, :],
@@ -264,46 +276,36 @@ def tile_linear_pa_kernel(tc, data, W, t_lora, lora_b, out):
                 nc.scalar.copy(out=tT[:], in_=bank[:])
             free_banks.append(b)
 
-        def quantize(key, halves, grp):
-            lo, hi = 256 * halves[0], 256 * (halves[-1] + 1)
-            if key[0] == "W":
-                codes = wq[:, key[1], key[2], lo:hi]
-                scales = ws[:, key[1], key[2], lo:hi]
-            else:
-                codes = dq[:, key[1], :, :].rearrange("p g r -> p (g r)")[:, lo:hi]
-                scales = ds[:, key[1], :, :].rearrange("p g r -> p (g r)")[:, lo:hi]
-            nc.vector.quantize_mx(out=codes.bitcast(E5X4), scales=scales, in_=grp[:, 4 * lo : 4 * hi])
-
         accs = {}
-        pls = {}
         deltas = {}
 
-        def matmul_item(item):
-            j, m = item[1], item[2]
-            if item[0] in ("PL", "PLa", "PLb"):
-                if item[0] != "PLb":
-                    pls[(j, m)] = take_bank([P, 512], F32, "pl")
-                bp, pl = pls[(j, m)]
-                lo = 256 if item[0] == "PLb" else 0
-                hi = 256 if item[0] == "PLa" else 512
-                nc.tensor.matmul(pl[:, lo:hi], lhsT=tT[:, m, :], rhs=lbT[:, m, j, lo:hi], start=True, stop=True)
-                if item[0] == "PLa":
-                    return
-                delta = stage.tile([P, 512], F32, name="delta", tag="delta", bufs=4)
-                nc.scalar.activation(
-                    out=delta[:].rearrange("s (p i) -> s p i", i=4),
-                    in_=pl[:].rearrange("s (i p) -> s p i", i=4),
-                    func=COPY,
-                    scale=2.0,
-                )
-                free_banks.append(bp)
-                deltas[(j, m)] = delta
-            else:
-                g = item[3]
-                if g == 0:
-                    accs[(j, m)] = take_bank([P, 512], F32, "acc")
+        def finish(unit, parts=1):
+            j, m = unit
+            ba, acc = accs[unit]
+            width = 512 // parts
+            for c in range(0, 512, width):
+                res = stage.tile([P, width], F32, name="res", tag="res", bufs=RES_BUFS)
+                nc.vector.tensor_tensor(out=res[:], in0=acc[:, c : c + width], in1=deltas[unit][:, c : c + width], op=ADD)
+                nc.sync.dma_start(out=out[m, :, 512 * j + c : 512 * j + c + width], in_=res[:])
+            free_banks.append(ba)
+
+        def matmuls(unit):
+            j, m = unit
+            bp, pl = take_bank([P, 512], F32, "pl")
+            nc.tensor.matmul(pl[:], lhsT=tT[:, m, :], rhs=lbT[:, m, j, :], start=True, stop=True)
+            delta = stage.tile([P, 512], F32, name="delta", tag="delta", bufs=6)
+            nc.scalar.activation(
+                out=delta[:].rearrange("s (p i) -> s p i", i=4),
+                in_=pl[:].rearrange("s (i p) -> s p i", i=4),
+                func=COPY,
+                scale=2.0,
+            )
+            free_banks.append(bp)
+            deltas[unit] = delta
+            accs[unit] = take_bank([P, 512], F32, "acc")
+            for g in range(NG):
                 nc.tensor.matmul_mx(
-                    out=accs[(j, m)][1][:],
+                    out=accs[unit][1][:],
                     lhsT=dq[:, m, g, :].bitcast(E5X4),
                     lhsT_scale=ds[:, m, g, :],
                     rhs=wq[:, j, g, :].bitcast(E5X4),
@@ -312,70 +314,41 @@ def tile_linear_pa_kernel(tc, data, W, t_lora, lora_b, out):
                     stop=(g == NG - 1),
                 )
 
-        def finish(unit, parts=1):
-            j, m = unit
-            ba, acc = accs[unit]
-            width = 512 // parts
-            for c in range(0, 512, width):
-                res = stage.tile([P, width], F32, name="res", tag="res", bufs=4)
-                nc.vector.tensor_tensor(out=res[:], in0=acc[:, c : c + width], in1=deltas[unit][:, c : c + width], op=ADD)
-                nc.sync.dma_start(out=out[m, :, 512 * j + c : 512 * j + c + width], in_=res[:])
-            free_banks.append(ba)
+        issue_ready_loads()
+        zeros = consts.tile([P, 512], BF16, name="zeros", tag="zeros")
+        nc.vector.memset(zeros[:], 0.0)
+        bw, warm = take_bank([P, 512], F32, "warm")
+        for n in range(WARM):
+            nc.tensor.matmul(warm[:], lhsT=zeros[:, 0:P], rhs=zeros[:], start=True, stop=True)
+        free_banks.append(bw)
 
-        issue_ready_loads(-1)
-        if WARM:
-            zeros = consts.tile([P, 512], BF16, name="zeros", tag="zeros")
-            nc.vector.memset(zeros[:], 0.0)
-            bw, warm = take_bank([P, 512], F32, "warm")
-            for n in range(WARM):
-                nc.tensor.matmul(warm[:], lhsT=zeros[:, 0:P], rhs=zeros[:], start=True, stop=True)
-            free_banks.append(bw)
-        sort_words(-1)
-        issue_ready_loads(-1)
         pending = []
-        closed = set()
-        for r, (bus, groups) in enumerate(rounds):
-            banks = [transposes(bu) for bu in bus]
-            for unit in pending:
-                finish(unit)
-            pending = []
-            if r >= VORDER_FROM:
-                sort_words(r)
-                issue_ready_loads(r)
-            pairs = {}
-            for k, bu in enumerate(bus):
-                grp, half, on_vector = None, 0, False
-                if bu[0] in ("W", "D"):
-                    key = bu[:-1]
-                    half = bu[-1]
-                    if key not in pairs:
-                        new = stage.tile([P, 2048], BF16, name="grp", tag="grp", bufs=5, align_bytes=64)
-                        pairs[key] = [new, [], False]
-                    grp = pairs[key][0]
-                    state["drains"] += 1
-                    on_vector = VEVERY > 0 and state["drains"] % VEVERY == 0
-                    pairs[key][1].append(half)
-                    pairs[key][2] = pairs[key][2] or on_vector
-                copy_out(bu, banks[k][0], banks[k][1], grp, half, on_vector)
-            for on_v in (False, True):
-                for key in pairs:
-                    if pairs[key][2] == on_v:
-                        quantize(key, pairs[key][1], pairs[key][0])
-            if r < VORDER_FROM:
-                sort_words(r)
-                issue_ready_loads(r)
-            for grp in groups:
-                for item in grp:
-                    matmul_item(item)
-                    if item[0] == "MX" and item[3] == NG - 1:
-                        closed.add((item[1], item[2]))
-                for unit in pending:
-                    finish(unit)
-                pending = []
-                for item in grp:
-                    unit = (item[1], item[2])
-                    if unit in closed and unit in deltas and unit not in pending:
-                        pending.append(unit)
-                        closed.remove(unit)
-        for unit in pending:
-            finish(unit, TAIL_PARTS)
+        for k, (kind, items) in enumerate(phases):
+            if kind == "run":
+                waiting = []
+                run_end = state["banks"] + len(items)
+                for bu in items:
+                    b, bank = transposes(bu)
+                    waiting.append((bu, b, bank))
+                    while len(waiting) > LAG:
+                        drain(waiting[0])
+                        waiting = waiting[1:]
+                    sort_words(len(unsorted_before(min(state["banks"] + AHEAD, run_end))))
+                    issue_ready_loads()
+                for entry in waiting:
+                    drain(entry)
+                quantize_but(0)
+            else:
+                next_run = len(phases[k + 1][1]) if k + 1 < len(phases) else 0
+                for n, unit in enumerate(items):
+                    matmuls(unit)
+                    for done in pending:
+                        finish(done)
+                    pending = [unit]
+                    todo = len(unsorted_before(state["banks"] + min(PRESORT, next_run)))
+                    left = len(items) - n
+                    sort_words((todo + left - 1) // left)
+                    issue_ready_loads()
+        for unit in pending[:-1]:
+            finish(unit)
+        finish(pending[-1], TAIL_PARTS)

@@ -19,8 +19,8 @@ IN = 2048
 FLOPS = 2 * 1024 * 2048 * 2048 + 2 * 1024 * 2048 * 128
 
 BUFS = {"raw": 8, "lraw": 8, "traw": 1}
-DEI_BUFS = 8
-RES_BUFS = 10
+DEI_BUFS = 7
+RES_BUFS = 6
 GRP_BUFS = 6
 WARM = 8
 VEVERY = 4
@@ -289,11 +289,12 @@ def tile_linear_pa_kernel(tc, data, W, t_lora, lora_b, out):
                 nc.sync.dma_start(out=out[m, :, 512 * j + c : 512 * j + c + width], in_=res[:])
             free_banks.append(ba)
 
-        def matmuls(unit):
+        def plain_product(unit):
             j, m = unit
             bp, pl = take_bank([P, 512], F32, "pl")
             nc.tensor.matmul(pl[:], lhsT=tT[:, m, :], rhs=lbT[:, m, j, :], start=True, stop=True)
-            delta = stage.tile([P, 512], F32, name="delta", tag="delta", bufs=6)
+            early = j == 1
+            delta = stage.tile([P, 512], F32, name="early" if early else "delta", tag="early" if early else "delta", bufs=NT if early else 4)
             nc.scalar.activation(
                 out=delta[:].rearrange("s (p i) -> s p i", i=4),
                 in_=pl[:].rearrange("s (i p) -> s p i", i=4),
@@ -302,6 +303,9 @@ def tile_linear_pa_kernel(tc, data, W, t_lora, lora_b, out):
             )
             free_banks.append(bp)
             deltas[unit] = delta
+
+        def mx_matmuls(unit):
+            j, m = unit
             accs[unit] = take_bank([P, 512], F32, "acc")
             for g in range(NG):
                 nc.tensor.matmul_mx(
@@ -341,7 +345,11 @@ def tile_linear_pa_kernel(tc, data, W, t_lora, lora_b, out):
             else:
                 next_run = len(phases[k + 1][1]) if k + 1 < len(phases) else 0
                 for n, unit in enumerate(items):
-                    matmuls(unit)
+                    if unit[0] != 1:
+                        plain_product(unit)
+                    if unit[0] == 0:
+                        plain_product((1, unit[1]))
+                    mx_matmuls(unit)
                     for done in pending:
                         finish(done)
                     pending = [unit]

from contextlib import ExitStack

import concourse.mybir as mybir
from concourse.masks import make_identity

F32 = mybir.dt.float32
BF16 = mybir.dt.bfloat16
U32 = mybir.dt.uint32
U8 = mybir.dt.uint8
E5X4 = mybir.dt.float8_e5m2_x4
COPY = mybir.ActivationFunctionType.Copy
ADD = mybir.AluOpType.add

P = 128
NT = 8
NC = 4
NG = 4
IN = 2048
FLOPS = 2 * 1024 * 2048 * 2048 + 2 * 1024 * 2048 * 128

BUFS = {"raw": 8, "lraw": 8, "traw": 1}
DEI_BUFS = 7
RES_BUFS = 6
GRP_BUFS = 6
WARM = 8
VEVERY = 4
LAG = 1
AHEAD = 4
PRESORT = 9
CUTS = [0, 1, 4, 7, 14, 22, 32]
HOLD = 2
TAIL_PARTS = 2


def w_banks(j):
    if j == 0:
        return [("W", j, g, h) for g in range(NG) for h in range(2)]
    return [("W", j, g, h) for h in range(2) for g in range(NG)]


def token_banks(m):
    return [("L", m, 0), ("D", m, 0), ("D", m, 1)]


def build_phases():
    units = [(j, m) for j in range(NC) for m in range(NT)]
    runs = [
        [("D", 0, 0), ("D", 0, 1)] + w_banks(0) + [("T",), ("L", 0, 0)] + token_banks(1),
        token_banks(2) + token_banks(3) + token_banks(4),
        token_banks(5) + token_banks(6) + token_banks(7),
        w_banks(1),
        w_banks(2) + [("L", m, 1) for m in range(NT)],
        w_banks(3),
    ]
    phases = []
    for n, run in enumerate(runs):
        phases.append(("run", run))
        phases.append(("block", units[CUTS[n] : CUTS[n + 1]]))
    return phases


def loads_of(bu):
    if bu[0] == "W" and bu[1] == 0:
        return [("w", 0, bu[2])]
    if bu[0] == "W":
        return [("w", bu[1], 2 * bu[3]), ("w", bu[1], 2 * bu[3] + 1)]
    if bu[0] == "D":
        return [("x", bu[1])]
    if bu[0] == "L":
        return [("l", bu[1], bu[2])]
    return [("t",)]


def tag_of(ld):
    return {"w": "raw", "x": "raw", "l": "lraw", "t": "traw"}[ld[0]]


def is_direct(ld):
    return ld[0] == "w" and ld[1] == 0 or ld[0] == "x" and ld[1] < 2


def tile_linear_pa_kernel(tc, data, W, t_lora, lora_b, out):
    nc = tc.nc
    phases = build_phases()

    seq = [bu for kind, items in phases if kind == "run" for bu in items]
    order = []
    first_use = {}
    last_use = {}
    for n, bu in enumerate(seq):
        for ld in loads_of(bu):
            if ld not in last_use:
                order.append(ld)
                first_use[ld] = n
            last_use[ld] = n
    by_tag = {"raw": [], "lraw": [], "traw": []}
    for ld in order:
        by_tag[tag_of(ld)].append(ld)
    word_loads = [ld for ld in order if tag_of(ld) == "raw" and not is_direct(ld)]

    with ExitStack() as ctx:
        consts = ctx.enter_context(tc.tile_pool(name="consts", bufs=1))
        keep = ctx.enter_context(tc.tile_pool(name="keep", bufs=1))
        raw = ctx.enter_context(tc.tile_pool(name="raw", bufs=2))
        stage = ctx.enter_context(tc.tile_pool(name="stage", bufs=2))
        psum = ctx.enter_context(tc.psum_pool(name="psum", bufs=1))

        ident_f = consts.tile([P, P], F32, name="ident_f", tag="ident_f")
        make_identity(nc, ident_f[:])
        ident_b = consts.tile([P, P], BF16, name="ident_b", tag="ident_b")
        make_identity(nc, ident_b[:])

        wq = keep.tile([P, NC, NG, 512], U32, name="wq", tag="wq", align_bytes=64)
        ws = keep.tile([P, NC, NG, 512], U8, name="ws", tag="ws", align_bytes=64)
        dq = keep.tile([P, NT, NG, P], U32, name="dq", tag="dq", align_bytes=64)
        ds = keep.tile([P, NT, NG, P], U8, name="ds", tag="ds", align_bytes=64)
        lbT = keep.tile([P, NT, NC, 512], BF16, name="lbT", tag="lbT")
        tT = keep.tile([P, NT, P], BF16, name="tT", tag="tT")

        ctx.enter_context(tc.manual_schedule())

        tiles = {}
        sorted_words = {}
        state = {"next_load": 0, "next_sort": 0, "banks": 0, "drains": 0}
        free_banks = list(range(8))

        def take_bank(shape, dtype, name):
            b = free_banks[0]
            free_banks.remove(b)
            return b, psum.tile(shape, dtype, name=name, tag="bank%d" % b)

        def issue_load(ld):
            kind = ld[0]
            if kind == "w" and ld[1] == 0:
                t = raw.tile([P, IN], BF16, name="raw", tag="raw", bufs=BUFS["raw"])
                nc.sync.dma_start(
                    out=t[:].rearrange("p (i k) -> p i k", i=4),
                    in_=W[0:512, 512 * ld[2] : 512 * (ld[2] + 1)].rearrange("(i p) k -> p i k", p=P),
                )
            elif kind == "w":
                t = raw.tile([P, IN], BF16, name="raw", tag="raw", bufs=BUFS["raw"])
                row = 512 * ld[1] + P * ld[2]
                nc.sync.dma_start(out=t[:], in_=W[row : row + P, :])
            elif kind == "x":
                t = raw.tile([P, IN], BF16, name="raw", tag="raw", bufs=BUFS["raw"])
                nc.sync.dma_start(out=t[:], in_=data[ld[1]])
            elif kind == "l":
                t = raw.tile([P, 2, 4, P], BF16, name="lraw", tag="lraw", bufs=BUFS["lraw"])
                src = lora_b[ld[1]].rearrange("(j p i) r -> p j (i r)", j=NC, p=P, i=4)
                nc.sync.dma_start(
                    out=t[:].rearrange("p j i r -> p j (i r)"),
                    in_=src[:, 2 * ld[2] : 2 * ld[2] + 2, :],
                )
            else:
                t = raw.tile([P, NT, P], BF16, name="traw", tag="traw", bufs=BUFS["traw"])
                nc.sync.dma_start(out=t[:], in_=t_lora.rearrange("a g s r -> s (a g) r"))
            tiles[ld] = t

        def released(ld):
            if ld in word_loads:
                return ld in sorted_words
            return last_use[ld] < state["banks"]

        def issue_ready_loads():
            while state["next_load"] < len(order):
                ld = order[state["next_load"]]
                peers = by_tag[tag_of(ld)]
                n = peers.index(ld)
                depth = BUFS[tag_of(ld)]
                if n >= depth and not released(peers[n - depth]):
                    break
                issue_load(ld)
                state["next_load"] += 1

        def unsorted_before(limit):
            return [ld for ld in word_loads[state["next_sort"] :] if first_use[ld] < limit]

        def sort_words(count):
            for c in range(count):
                n = state["next_sort"]
                if n >= len(word_loads) or word_loads[n] not in tiles:
                    break
                if n >= DEI_BUFS and last_use[word_loads[n - DEI_BUFS]] >= state["banks"]:
                    break
                ld = word_loads[n]
                dei = stage.tile([P, NG, 2, P], F32, name="dei", tag="dei", bufs=DEI_BUFS)
                nc.vector.tensor_copy(
                    out=dei[:],
                    in_=tiles[ld][:].bitcast(F32).rearrange("r (g p u) -> r g u p", g=NG, u=2),
                )
                sorted_words[ld] = dei
                state["next_sort"] += 1
            issue_ready_loads()

        def words_of(ld, n, u):
            if is_direct(ld):
                return tiles[ld][:].bitcast(F32)[:, 256 * n + u : 256 * (n + 1) : 2]
            return sorted_words[ld][:, n, u, :]

        def transposes(bu):
            kind = bu[0]
            if kind == "W" or kind == "D":
                b, bank = take_bank([P, 2, 2, P], F32, "trf")
                for a in range(2):
                    if kind == "W" and bu[1] == 0:
                        ld, n = ("w", 0, bu[2]), 2 * bu[3] + a
                    elif kind == "W":
                        ld, n = ("w", bu[1], 2 * bu[3] + a), bu[2]
                    else:
                        ld, n = ("x", bu[1]), 2 * bu[2] + a
                    for u in range(2):
                        nc.tensor.transpose(bank[:, a, u, :], words_of(ld, n, u), ident_f[:])
            elif kind == "L":
                b, bank = take_bank([P, 2, 4, P], BF16, "trl")
                src = tiles[("l", bu[1], bu[2])]
                for jj in range(2):
                    for i in range(4):
                        nc.tensor.transpose(bank[:, jj, i, :], src[:, jj, i, :], ident_b[:])
            else:
                b, bank = take_bank([P, NT, P], BF16, "trt")
                src = tiles[("t",)]
                for m in range(NT):
                    nc.tensor.transpose(bank[:, m, :], src[:, m, :], ident_b[:])
            state["banks"] += 1
            return b, bank

        pairs = {}
        full_pairs = []

        def quantize(key):
            grp = pairs[key]
            if key[0] == "W" and len(key) == 4:
                lo = 256 * key[3]
                codes = wq[:, key[1], key[2], lo : lo + 256]
                scales = ws[:, key[1], key[2], lo : lo + 256]
            elif key[0] == "W":
                codes = wq[:, key[1], key[2], :]
                scales = ws[:, key[1], key[2], :]
            else:
                codes = dq[:, key[1], :, :].rearrange("p g r -> p (g r)")
                scales = ds[:, key[1], :, :].rearrange("p g r -> p (g r)")
            nc.vector.quantize_mx(out=codes.bitcast(E5X4), scales=scales, in_=grp[:])

        def quantize_but(keep_back):
            while len(full_pairs) > keep_back:
                quantize(full_pairs[0])
                full_pairs.remove(full_pairs[0])

        def drain(entry):
            bu, b, bank = entry
            kind = bu[0]
            if kind == "W" or kind == "D":
                alone = kind == "W" and bu[1] > 0
                key = bu if alone else bu[:-1]
                half = 0 if alone else bu[-1]
                if half == 0:
                    width = 1024 if alone else 2048
                    pairs[key] = stage.tile([P, width], BF16, name="grp", tag="grp", bufs=GRP_BUFS, align_bytes=64)
                grp = pairs[key]
                dst = grp[:, 1024 * half : 1024 * (half + 1)].bitcast(F32).rearrange("p (a r u) -> p a r u", a=2, u=2)
                src = bank[:].rearrange("p a u r -> p a r u")
                state["drains"] += 1
                if state["drains"] % VEVERY == 0:
                    nc.vector.tensor_copy(out=dst, in_=src)
                else:
                    nc.scalar.copy(out=dst, in_=src)
                if half == 1 or alone:
                    full_pairs.append(key)
                    quantize_but(1)
            elif kind == "L":
                nc.scalar.copy(
                    out=lbT[:, bu[1], 2 * bu[2] : 2 * bu[2] + 2, :],
                    in_=bank[:].rearrange("r j i p -> r j (i p)"),
                )
            else:
                nc.scalar.copy(out=tT[:], in_=bank[:])
            free_banks.append(b)

        accs = {}
        deltas = {}

        def finish(unit, parts=1):
            j, m = unit
            ba, acc = accs[unit]
            width = 512 // parts
            for c in range(0, 512, width):
                res = stage.tile([P, width], F32, name="res", tag="res", bufs=RES_BUFS)
                nc.vector.tensor_tensor(out=res[:], in0=acc[:, c : c + width], in1=deltas[unit][:, c : c + width], op=ADD)
                nc.sync.dma_start(out=out[m, :, 512 * j + c : 512 * j + c + width], in_=res[:])
            free_banks.append(ba)

        def plain_product(unit):
            j, m = unit
            bp, pl = take_bank([P, 512], F32, "pl")
            nc.tensor.matmul(pl[:], lhsT=tT[:, m, :], rhs=lbT[:, m, j, :], start=True, stop=True)
            early = j == 1
            delta = stage.tile([P, 512], F32, name="early" if early else "delta", tag="early" if early else "delta", bufs=NT if early else 4)
            nc.scalar.activation(
                out=delta[:].rearrange("s (p i) -> s p i", i=4),
                in_=pl[:].rearrange("s (i p) -> s p i", i=4),
                func=COPY,
                scale=2.0,
            )
            free_banks.append(bp)
            deltas[unit] = delta

        def mx_matmuls(unit):
            j, m = unit
            accs[unit] = take_bank([P, 512], F32, "acc")
            for g in range(NG):
                nc.tensor.matmul_mx(
                    out=accs[unit][1][:],
                    lhsT=dq[:, m, g, :].bitcast(E5X4),
                    lhsT_scale=ds[:, m, g, :],
                    rhs=wq[:, j, g, :].bitcast(E5X4),
                    rhs_scale=ws[:, j, g, :],
                    start=(g == 0),
                    stop=(g == NG - 1),
                )

        issue_ready_loads()
        zeros = consts.tile([P, 512], BF16, name="zeros", tag="zeros")
        nc.vector.memset(zeros[:], 0.0)
        bw, warm = take_bank([P, 512], F32, "warm")
        for n in range(WARM):
            nc.tensor.matmul(warm[:], lhsT=zeros[:, 0:P], rhs=zeros[:], start=True, stop=True)
        free_banks.append(bw)

        pending = []
        for k, (kind, items) in enumerate(phases):
            if kind == "run":
                waiting = []
                run_end = state["banks"] + len(items)
                for bu in items:
                    b, bank = transposes(bu)
                    waiting.append((bu, b, bank))
                    while len(waiting) > LAG:
                        drain(waiting[0])
                        waiting = waiting[1:]
                    sort_words(len(unsorted_before(min(state["banks"] + AHEAD, run_end))))
                    issue_ready_loads()
                for entry in waiting:
                    drain(entry)
                quantize_but(0)
            else:
                next_run = len(phases[k + 1][1]) if k + 1 < len(phases) else 0
                for n, unit in enumerate(items):
                    if unit[0] != 1:
                        plain_product(unit)
                    if unit[0] == 0:
                        plain_product((1, unit[1]))
                    mx_matmuls(unit)
                    for done in pending:
                        finish(done)
                    pending = [unit]
                    todo = len(unsorted_before(state["banks"] + min(PRESORT, next_run)))
                    left = len(items) - n
                    sort_words((todo + left - 1) // left)
                    issue_ready_loads()
        for unit in pending[:-1]:
            finish(unit)
        finish(pending[-1], TAIL_PARTS)
